import numpy as np
import ml_dtypes


def mxq(x, axis, fmt="e4m3"):
    dtype, down = {"e4m3": (ml_dtypes.float8_e4m3fn, 7), "e5m2": (ml_dtypes.float8_e5m2, 14)}[fmt]
    v = np.moveaxis(np.asarray(x, np.float32).astype(ml_dtypes.bfloat16).astype(np.float64), axis, -1)
    blocks = v.reshape(v.shape[:-1] + (-1, 32))
    amax = np.abs(blocks).max(-1, keepdims=True)
    byte = np.maximum(np.where(amax > 0, np.frexp(amax)[1] - 1 + 127, 0) - down, 1)
    scale = np.exp2(byte - 127.0)
    codes = (blocks / scale).astype(np.float32).astype(dtype).astype(np.float64)
    return np.moveaxis((codes * scale).reshape(v.shape), -1, axis)


WIDE = False


def mx_kscale(k):
    if not WIDE:
        return np.ones(k)
    levels = np.array([10, -10, 5, -5, 0])
    if k % 512:
        return np.exp2(np.random.permutation(np.resize(levels, k // 32))).repeat(32)
    a = np.empty((k // 512, 16))
    for p in range(k // 512):
        a[p, :8] = np.random.permutation(np.resize(levels, 8))
        for g in range(8):
            far = levels[np.abs(levels - a[p, g]) >= 10]
            a[p, g + 8] = far[np.random.randint(len(far))]
    return np.exp2(a.ravel()).repeat(32)


BF16 = ml_dtypes.bfloat16


def bf(x):
    return np.asarray(x, np.float32).astype(BF16)


def f64(x):
    return np.asarray(x).astype(np.float64)


B, P, K, D, L, C0, C1, C2, C3 = 1024, 64, 128, 256, 4, 64, 128, 256, 512
C = C3
F = 2 * C
EPS = 1e-5


def layernorm(x, g, b):
    m = x.mean(axis=-1, keepdims=True)
    v = x.var(axis=-1, keepdims=True)
    return (x - m) / np.sqrt(v + EPS) * g + b


def l2norm(x):
    n = np.sqrt((x * x).sum(axis=-1, keepdims=True))
    return x / np.maximum(n, 1e-12)


def setup_inputs():
    s = mx_kscale(F)
    return {"pooled": bf(0.5 + 2.0 * np.random.standard_normal((B, C))),
            "proto": bf(np.random.standard_normal((1, C)) + np.random.standard_normal((P, C))),
            "ln_g": bf((1.0 + 0.1 * np.random.standard_normal(F)) * s),
            "ln_b": bf(0.1 * np.random.standard_normal(F) * s),
            "W": bf(np.random.standard_normal((F, D)) / np.sqrt(F) / s[:, None]),
            "b": bf(0.1 * np.random.standard_normal(D))}


def reference(pooled, proto, ln_g, ln_b, W, b):
    pl = f64(pooled)
    proto_ctx = np.broadcast_to(f64(proto).mean(axis=0, keepdims=True), pl.shape)
    fused = np.concatenate([pl, proto_ctx], axis=1)
    z = layernorm(fused, f64(ln_g), f64(ln_b))
    h = np.maximum((mxq(z, 1, "e4m3") @ mxq(f64(W), 0, "e4m3")) + f64(b), 0.0)
    return l2norm(h)

@@ -1,0 +1,255 @@
+from contextlib import ExitStack
+
+import concourse.mybir as mybir
+from concourse.masks import make_identity
+
+F32 = mybir.dt.float32
+BF16 = mybir.dt.bfloat16
+U32 = mybir.dt.uint32
+U8 = mybir.dt.uint8
+FP8X4 = mybir.dt.float8_e4m3fn_x4
+ALU = mybir.AluOpType
+ACT = mybir.ActivationFunctionType
+
+P = 128
+PACK = 4
+ROWS = 1024
+C = 512
+HALVES = 2
+POOLED, PROTO = 0, 1
+D = 256
+PROTOS = 64
+TILES = ROWS // P
+GROUP = 2
+GROUPS = TILES // GROUP
+GROUP_ROWS = GROUP * P
+K_BLOCKS = HALVES * PACK
+BANK_BLOCKS = 2
+STATS = 6
+EPS = 1e-5
+SKEW = 2
+FLOPS = 2 * ROWS * HALVES * C * D
+
+
+def tile_textguidedcamfusion_pa_s_kernel(tc, pooled, proto, ln_g, ln_b, W, b, out):
+    nc = tc.nc
+    with ExitStack() as ctx:
+        keep = ctx.enter_context(tc.tile_pool(name="keep", bufs=1))
+        scratch = ctx.enter_context(tc.tile_pool(name="scratch", bufs=2))
+        banks = ctx.enter_context(tc.psum_pool(name="banks", bufs=5))
+        products = ctx.enter_context(tc.psum_pool(name="products", bufs=2))
+
+        g_raw = keep.tile([P, HALVES, PACK], BF16)
+        s_raw = keep.tile([P, HALVES, PACK], BF16)
+        bias_pad = keep.tile([P, D], BF16)
+        nc.vector.memset(bias_pad[:], 0.0)
+        proto_pad = keep.tile([P, C], BF16)
+        nc.vector.memset(proto_pad[PROTOS:P, :], 0.0)
+        nc.scalar.dma_start(out=g_raw[:], in_=ln_g.rearrange("(h p t) -> p h t", p=P, t=PACK))
+        nc.scalar.dma_start(out=s_raw[:], in_=ln_b.rearrange("(h p t) -> p h t", p=P, t=PACK))
+        nc.scalar.dma_start(out=bias_pad[0:1, :], in_=b.rearrange("(o d) -> o d", o=1))
+        x = keep.tile([P, TILES, C], BF16)
+        pooled_rows = pooled.rearrange("(p j) c -> p j c", j=TILES)
+        out_rows = out.rearrange("(p j) d -> p j d", j=TILES)
+        w_raw = keep.tile([P, K_BLOCKS, D], BF16)
+        nc.sync.dma_start(out=proto_pad[0:PROTOS, :], in_=proto)
+        nc.sync.dma_start(out=x[:, 0:GROUP, :], in_=pooled_rows[:, 0:GROUP, :])
+        nc.sync.dma_start(out=x[:, GROUP : 2 * GROUP, :], in_=pooled_rows[:, GROUP : 2 * GROUP, :])
+        nc.sync.dma_start(
+            out=w_raw[:].rearrange("p (h t) d -> p h (t d)", t=PACK),
+            in_=W.rearrange("(h p t) d -> p h (t d)", p=P, t=PACK),
+        )
+        nc.sync.dma_start(out=x[:, 2 * GROUP : TILES, :], in_=pooled_rows[:, 2 * GROUP : TILES, :])
+
+        eps_col = keep.tile([P, 1], F32)
+        nc.vector.memset(eps_col[:], EPS)
+        warm = keep.tile([P, 1], F32)
+        nc.scalar.sqrt(out=warm[:], in_=eps_col[:])
+        mean_weights = keep.tile([P, P], BF16)
+        nc.vector.memset(mean_weights[:], 1.0 / PROTOS)
+        ones = keep.tile([P, P], BF16)
+        nc.vector.memset(ones[:], 1.0)
+        ident = keep.tile([P, P], F32)
+        make_identity(nc, ident[:])
+        gain = keep.tile([P, HALVES, PACK], F32)
+        offset = keep.tile([P, HALVES, PACK], F32)
+        nc.gpsimd.tensor_copy(out=gain[:], in_=g_raw[:])
+        nc.gpsimd.tensor_copy(out=offset[:], in_=s_raw[:])
+
+        c_bank = banks.tile([P, C], F32, tag="bank")
+        nc.tensor.matmul(out=c_bank[:], lhsT=mean_weights[:], rhs=proto_pad[:], start=True, stop=True)
+        c_all = keep.tile([P, PACK, P], F32)
+        nc.scalar.copy(out=c_all[:], in_=c_bank[:].rearrange("p (q t) -> p t q", t=PACK))
+
+        stats = keep.tile([P, TILES, HALVES, STATS], F32)
+        c_stats = keep.tile([P, STATS], F32)
+        mean_var = keep.tile([P, TILES, 2], F32)
+        std = keep.tile([P, TILES], F32)
+        rstd = keep.tile([P, TILES], F32)
+        shift = keep.tile([P, TILES], F32)
+        y = keep.tile([P, TILES, HALVES, PACK, P], F32)
+        y_t = {}
+        planes = keep.tile([P, GROUPS, HALVES, PACK, GROUP_ROWS], BF16)
+        z_grouped = keep.tile([P, GROUPS, HALVES, GROUP_ROWS, PACK], BF16, align_bytes=64)
+        z_codes = keep.tile([P, GROUPS, HALVES, GROUP_ROWS], U32, align_bytes=64)
+        z_scales = keep.tile([P, GROUPS, HALVES, GROUP_ROWS], U8, align_bytes=64)
+        w_grouped = keep.tile([P, HALVES, D, PACK], BF16, align_bytes=64)
+        w_codes = keep.tile([P, HALVES, D], U32, align_bytes=64)
+        w_scales = keep.tile([P, HALVES, D], U8, align_bytes=64)
+        b_all = keep.tile([P, D], F32)
+        acc = {}
+        pre = keep.tile([P, TILES, D], F32)
+        sumsq = keep.tile([P, TILES], F32)
+        norm = keep.tile([P, TILES], F32)
+        rnorm = keep.tile([P, TILES], F32)
+        result = keep.tile([P, TILES, D], F32)
+
+        def tiles_of(g):
+            return range(GROUP * g, GROUP * (g + 1))
+
+        def cols_of(g):
+            return slice(GROUP * g, GROUP * (g + 1))
+
+        def row_moments(g):
+            for j in tiles_of(g):
+                nc.vector.bn_stats(out=stats[:, j, POOLED, :], in_=x[:, j, :])
+
+        def join_moments(g):
+            for j in tiles_of(g):
+                nc.vector.bn_aggr(out=mean_var[:, j, :], in_=stats[:, j].rearrange("p h s -> p (h s)"))
+
+        def std_of(g):
+            nc.scalar.activation(out=std[:, cols_of(g)], in_=mean_var[:, cols_of(g), 1], func=ACT.Sqrt, bias=eps_col[:])
+
+        def rstd_of(g):
+            nc.vector.reciprocal(out=rstd[:, cols_of(g)], in_=std[:, cols_of(g)])
+
+        def shift_of(g):
+            nc.vector.scalar_tensor_tensor(
+                out=shift[:, cols_of(g)], in0=mean_var[:, cols_of(g), 0], scalar=-1.0, in1=rstd[:, cols_of(g)],
+                op0=ALU.mult, op1=ALU.mult,
+            )
+
+        def transpose_half(g, h):
+            for u in range(PACK // BANK_BLOCKS):
+                y_t[(g, h, u)] = banks.tile([P, BANK_BLOCKS, GROUP_ROWS], F32, tag="bank", name="y_t")
+                for v in range(BANK_BLOCKS):
+                    t = BANK_BLOCKS * u + v
+                    for e, j in enumerate(tiles_of(g)):
+                        nc.tensor.transpose(
+                            y_t[(g, h, u)][:, v, P * e : P * (e + 1)], y[:, j, h, t, :], ident[:]
+                        )
+
+        def normalise(g):
+            for j in tiles_of(g):
+                nc.scalar.activation(
+                    out=y[:, j, POOLED], in_=x[:, j, :].rearrange("p (q t) -> p t q", t=PACK), func=ACT.Identity,
+                    scale=rstd[:, j : j + 1], bias=shift[:, j : j + 1],
+                )
+                nc.vector.tensor_scalar(
+                    out=y[:, j, PROTO], in0=c_all[:], scalar1=rstd[:, j : j + 1], scalar2=shift[:, j : j + 1],
+                    op0=ALU.mult, op1=ALU.add,
+                )
+
+        def transpose(g):
+            for h in range(HALVES):
+                transpose_half(g, h)
+
+        def gain_and_shift(g):
+            for kb in range(K_BLOCKS):
+                h, t = divmod(kb, PACK)
+                nc.scalar.activation(
+                    out=planes[:, g, h, t, :], in_=y_t[(g, h, t // BANK_BLOCKS)][:, t % BANK_BLOCKS, :],
+                    func=ACT.Identity, scale=gain[:, h, t : t + 1], bias=offset[:, h, t : t + 1],
+                )
+
+        def regroup(g):
+            for h in range(HALVES):
+                nc.vector.tensor_copy(
+                    out=z_grouped[:, g, h].rearrange("p (c i) t -> p c t i", i=4),
+                    in_=planes[:, g, h].rearrange("p t (c i) -> p c t i", i=4),
+                )
+
+        def quantise(g):
+            for h in range(HALVES):
+                nc.vector.quantize_mx(
+                    out=z_codes[:, g, h, :].bitcast(FP8X4),
+                    scales=z_scales[:, g, h, :],
+                    in_=z_grouped[:, g, h].rearrange("p r t -> p (r t)"),
+                )
+
+        def regroup_w(h):
+            nc.gpsimd.tensor_scalar(
+                out=w_grouped[:, h].rearrange("p (c i) t -> p c t i", i=4),
+                in0=w_raw[:, PACK * h : PACK * (h + 1), :].rearrange("p t (c i) -> p c t i", i=4),
+                scalar1=1.0, scalar2=0.0, op0=ALU.mult, op1=ALU.add,
+            )
+
+        def quantise_w():
+            nc.vector.quantize_mx(
+                out=w_codes[:].rearrange("p h d -> p (h d)").bitcast(FP8X4),
+                scales=w_scales[:].rearrange("p h d -> p (h d)"),
+                in_=w_grouped[:].rearrange("p h d t -> p (h d t)"),
+            )
+
+        def project(g):
+            acc[g] = products.tile([P, GROUP, D], F32, name="acc")
+            for e in range(GROUP):
+                rows = slice(P * e, P * (e + 1))
+                for h in range(HALVES):
+                    nc.tensor.matmul_mx(
+                        out=acc[g][:, e, :],
+                        lhsT=z_codes[:, g, h, rows].bitcast(FP8X4),
+                        lhsT_scale=z_scales[:, g, h, rows],
+                        rhs=w_codes[:, h, :].bitcast(FP8X4),
+                        rhs_scale=w_scales[:, h, :],
+                        start=(h == 0),
+                        stop=(h == HALVES - 1),
+                    )
+
+        def add_bias(g):
+            nc.vector.tensor_tensor(
+                out=pre[:, cols_of(g), :], in0=acc[g][:],
+                in1=b_all[:].unsqueeze(1).to_broadcast([P, GROUP, D]), op=ALU.add,
+            )
+
+        def sum_squares(g):
+            for j in tiles_of(g):
+                squares = scratch.tile([P, D], F32)
+                nc.vector.scalar_tensor_tensor(
+                    out=squares[:], in0=pre[:, j, :], scalar=0.0, in1=pre[:, j, :],
+                    op0=ALU.max, op1=ALU.mult, accum_out=sumsq[:, j : j + 1],
+                )
+
+        def floor_sumsq(g):
+            nc.vector.tensor_scalar_max(out=norm[:, cols_of(g)], in0=sumsq[:, cols_of(g)], scalar1=1e-24)
+
+        def norm_of(g):
+            nc.scalar.sqrt(out=norm[:, cols_of(g)], in_=norm[:, cols_of(g)])
+
+        def rnorm_of(g):
+            nc.vector.reciprocal(out=rnorm[:, cols_of(g)], in_=norm[:, cols_of(g)])
+
+        def scale_and_store(g):
+            for j in tiles_of(g):
+                nc.scalar.activation(out=result[:, j, :], in_=pre[:, j, :], func=ACT.Relu, scale=rnorm[:, j : j + 1])
+            nc.sync.dma_start(out=out_rows[:, cols_of(g), :], in_=result[:, cols_of(g), :])
+
+        nc.vector.bn_stats(out=c_stats[:], in_=c_bank[:])
+        nc.vector.tensor_copy(out=stats[:, :, PROTO, :], in_=c_stats[:].unsqueeze(1).to_broadcast([P, TILES, STATS]))
+        b_bank = banks.tile([P, D], F32, tag="bank")
+        nc.tensor.matmul(out=b_bank[:], lhsT=ones[:], rhs=bias_pad[:], start=True, stop=True)
+        nc.scalar.copy(out=b_all[:], in_=b_bank[:])
+        for h in range(HALVES):
+            regroup_w(h)
+        quantise_w()
+
+        stages = [
+            row_moments, join_moments, std_of, rstd_of, shift_of, normalise, transpose, gain_and_shift, regroup,
+            quantise, project, add_bias, sum_squares, floor_sumsq, norm_of, rnorm_of, scale_and_store,
+        ]
+        for wave in range(len(stages) + SKEW * (GROUPS - 1)):
+            for g in range(GROUPS):
+                s = wave - SKEW * g
+                if 0 <= s < len(stages):
+                    stages[s](g)

@@ -20,14 +20,8 @@ POOLED, PROTO = 0, 1
 D = 256
 PROTOS = 64
 TILES = ROWS // P
-GROUP = 2
-GROUPS = TILES // GROUP
-GROUP_ROWS = GROUP * P
-K_BLOCKS = HALVES * PACK
-BANK_BLOCKS = 2
 STATS = 6
 EPS = 1e-5
-SKEW = 2
 FLOPS = 2 * ROWS * HALVES * C * D
 
 
@@ -35,40 +29,45 @@ def tile_textguidedcamfusion_pa_s_kernel(tc, pooled, proto, ln_g, ln_b, W, b, ou
     nc = tc.nc
     with ExitStack() as ctx:
         keep = ctx.enter_context(tc.tile_pool(name="keep", bufs=1))
-        scratch = ctx.enter_context(tc.tile_pool(name="scratch", bufs=2))
-        banks = ctx.enter_context(tc.psum_pool(name="banks", bufs=5))
+        banks = ctx.enter_context(tc.psum_pool(name="banks", bufs=6))
         products = ctx.enter_context(tc.psum_pool(name="products", bufs=2))
+        ctx.enter_context(tc.manual_schedule())
 
-        g_raw = keep.tile([P, HALVES, PACK], BF16)
-        s_raw = keep.tile([P, HALVES, PACK], BF16)
-        bias_pad = keep.tile([P, D], BF16)
-        nc.vector.memset(bias_pad[:], 0.0)
         proto_pad = keep.tile([P, C], BF16)
-        nc.vector.memset(proto_pad[PROTOS:P, :], 0.0)
-        nc.scalar.dma_start(out=g_raw[:], in_=ln_g.rearrange("(h p t) -> p h t", p=P, t=PACK))
-        nc.scalar.dma_start(out=s_raw[:], in_=ln_b.rearrange("(h p t) -> p h t", p=P, t=PACK))
-        nc.scalar.dma_start(out=bias_pad[0:1, :], in_=b.rearrange("(o d) -> o d", o=1))
+        nc.sync.dma_start(out=proto_pad[0:PROTOS, :], in_=proto)
         x = keep.tile([P, TILES, C], BF16)
         pooled_rows = pooled.rearrange("(p j) c -> p j c", j=TILES)
         out_rows = out.rearrange("(p j) d -> p j d", j=TILES)
-        w_raw = keep.tile([P, K_BLOCKS, D], BF16)
-        nc.sync.dma_start(out=proto_pad[0:PROTOS, :], in_=proto)
-        nc.sync.dma_start(out=x[:, 0:GROUP, :], in_=pooled_rows[:, 0:GROUP, :])
-        nc.sync.dma_start(out=x[:, GROUP : 2 * GROUP, :], in_=pooled_rows[:, GROUP : 2 * GROUP, :])
+
+        def load_x(a, z):
+            nc.sync.dma_start(out=x[:, a:z, :], in_=pooled_rows[:, a:z, :])
+
+        load_x(0, 1)
+        load_x(1, 2)
+        w_raw = keep.tile([P, HALVES * PACK, D], BF16)
         nc.sync.dma_start(
             out=w_raw[:].rearrange("p (h t) d -> p h (t d)", t=PACK),
             in_=W.rearrange("(h p t) d -> p h (t d)", p=P, t=PACK),
         )
-        nc.sync.dma_start(out=x[:, 2 * GROUP : TILES, :], in_=pooled_rows[:, 2 * GROUP : TILES, :])
+        load_x(2, 4)
+        load_x(4, TILES)
+        g_raw = keep.tile([P, HALVES, PACK], BF16)
+        s_raw = keep.tile([P, HALVES, PACK], BF16)
+        bias_pad = keep.tile([P, D], BF16)
 
-        eps_col = keep.tile([P, 1], F32)
-        nc.vector.memset(eps_col[:], EPS)
-        warm = keep.tile([P, 1], F32)
-        nc.scalar.sqrt(out=warm[:], in_=eps_col[:])
+        nc.vector.memset(proto_pad[PROTOS:P, :], 0.0)
         mean_weights = keep.tile([P, P], BF16)
         nc.vector.memset(mean_weights[:], 1.0 / PROTOS)
+        eps_col = keep.tile([P, 1], F32)
+        nc.vector.memset(eps_col[:], EPS)
         ones = keep.tile([P, P], BF16)
         nc.vector.memset(ones[:], 1.0)
+        nc.vector.memset(bias_pad[:], 0.0)
+        nc.scalar.dma_start(out=g_raw[:], in_=ln_g.rearrange("(h p t) -> p h t", p=P, t=PACK))
+        nc.scalar.dma_start(out=s_raw[:], in_=ln_b.rearrange("(h p t) -> p h t", p=P, t=PACK))
+        nc.scalar.dma_start(out=bias_pad[0:1, :], in_=b.rearrange("(o d) -> o d", o=1))
+        warm = keep.tile([P, 1], F32)
+        nc.scalar.activation(out=warm[:], in_=eps_col[:], func=ACT.Abs_reciprocal_sqrt)
         ident = keep.tile([P, P], F32)
         make_identity(nc, ident[:])
         gain = keep.tile([P, HALVES, PACK], F32)
@@ -76,112 +75,78 @@ def tile_textguidedcamfusion_pa_s_kernel(tc, pooled, proto, ln_g, ln_b, W, b, ou
         nc.gpsimd.tensor_copy(out=gain[:], in_=g_raw[:])
         nc.gpsimd.tensor_copy(out=offset[:], in_=s_raw[:])
 
-        c_bank = banks.tile([P, C], F32, tag="bank")
-        nc.tensor.matmul(out=c_bank[:], lhsT=mean_weights[:], rhs=proto_pad[:], start=True, stop=True)
         c_all = keep.tile([P, PACK, P], F32)
-        nc.scalar.copy(out=c_all[:], in_=c_bank[:].rearrange("p (q t) -> p t q", t=PACK))
-
         stats = keep.tile([P, TILES, HALVES, STATS], F32)
-        c_stats = keep.tile([P, STATS], F32)
         mean_var = keep.tile([P, TILES, 2], F32)
-        std = keep.tile([P, TILES], F32)
         rstd = keep.tile([P, TILES], F32)
-        shift = keep.tile([P, TILES], F32)
         y = keep.tile([P, TILES, HALVES, PACK, P], F32)
         y_t = {}
-        planes = keep.tile([P, GROUPS, HALVES, PACK, GROUP_ROWS], BF16)
-        z_grouped = keep.tile([P, GROUPS, HALVES, GROUP_ROWS, PACK], BF16, align_bytes=64)
-        z_codes = keep.tile([P, GROUPS, HALVES, GROUP_ROWS], U32, align_bytes=64)
-        z_scales = keep.tile([P, GROUPS, HALVES, GROUP_ROWS], U8, align_bytes=64)
+        planes = keep.tile([P, TILES, PACK, HALVES * P], BF16)
+        z_grouped = keep.tile([P, TILES, HALVES * P, PACK], BF16, align_bytes=64)
+        z_codes = keep.tile([P, TILES, HALVES * P], U32, align_bytes=64)
+        z_scales = keep.tile([P, TILES, HALVES * P], U8, align_bytes=64)
         w_grouped = keep.tile([P, HALVES, D, PACK], BF16, align_bytes=64)
         w_codes = keep.tile([P, HALVES, D], U32, align_bytes=64)
         w_scales = keep.tile([P, HALVES, D], U8, align_bytes=64)
         b_all = keep.tile([P, D], F32)
         acc = {}
         pre = keep.tile([P, TILES, D], F32)
+        h = keep.tile([P, TILES, D], F32)
+        squares = keep.tile([P, D], F32)
         sumsq = keep.tile([P, TILES], F32)
-        norm = keep.tile([P, TILES], F32)
         rnorm = keep.tile([P, TILES], F32)
+        rfloor = {j: keep.tile([P, 1], F32, name="rfloor_" + str(j)) for j in range(TILES)}
         result = keep.tile([P, TILES, D], F32)
 
-        def tiles_of(g):
-            return range(GROUP * g, GROUP * (g + 1))
+        def row_stats(j):
+            nc.vector.bn_stats(out=stats[:, j, POOLED, :], in_=x[:, j, :])
 
-        def cols_of(g):
-            return slice(GROUP * g, GROUP * (g + 1))
+        def join_stats(j):
+            nc.vector.bn_aggr(out=mean_var[:, j, :], in_=stats[:, j].rearrange("p h s -> p (h s)"))
 
-        def row_moments(g):
-            for j in tiles_of(g):
-                nc.vector.bn_stats(out=stats[:, j, POOLED, :], in_=x[:, j, :])
-
-        def join_moments(g):
-            for j in tiles_of(g):
-                nc.vector.bn_aggr(out=mean_var[:, j, :], in_=stats[:, j].rearrange("p h s -> p (h s)"))
-
-        def std_of(g):
-            nc.scalar.activation(out=std[:, cols_of(g)], in_=mean_var[:, cols_of(g), 1], func=ACT.Sqrt, bias=eps_col[:])
-
-        def rstd_of(g):
-            nc.vector.reciprocal(out=rstd[:, cols_of(g)], in_=std[:, cols_of(g)])
-
-        def shift_of(g):
-            nc.vector.scalar_tensor_tensor(
-                out=shift[:, cols_of(g)], in0=mean_var[:, cols_of(g), 0], scalar=-1.0, in1=rstd[:, cols_of(g)],
-                op0=ALU.mult, op1=ALU.mult,
+        def rstd_of(j):
+            nc.scalar.activation(
+                out=rstd[:, j : j + 1], in_=mean_var[:, j, 1:2], func=ACT.Abs_reciprocal_sqrt, bias=eps_col[:]
             )
 
-        def transpose_half(g, h):
-            for u in range(PACK // BANK_BLOCKS):
-                y_t[(g, h, u)] = banks.tile([P, BANK_BLOCKS, GROUP_ROWS], F32, tag="bank", name="y_t")
-                for v in range(BANK_BLOCKS):
-                    t = BANK_BLOCKS * u + v
-                    for e, j in enumerate(tiles_of(g)):
-                        nc.tensor.transpose(
-                            y_t[(g, h, u)][:, v, P * e : P * (e + 1)], y[:, j, h, t, :], ident[:]
-                        )
-
-        def normalise(g):
-            for j in tiles_of(g):
-                nc.scalar.activation(
-                    out=y[:, j, POOLED], in_=x[:, j, :].rearrange("p (q t) -> p t q", t=PACK), func=ACT.Identity,
-                    scale=rstd[:, j : j + 1], bias=shift[:, j : j + 1],
-                )
+        def normalise(j):
+            sources = (x[:, j, :].rearrange("p (q t) -> p t q", t=PACK), c_all[:])
+            for half in range(HALVES):
                 nc.vector.tensor_scalar(
-                    out=y[:, j, PROTO], in0=c_all[:], scalar1=rstd[:, j : j + 1], scalar2=shift[:, j : j + 1],
-                    op0=ALU.mult, op1=ALU.add,
+                    out=y[:, j, half], in0=sources[half], scalar1=mean_var[:, j, 0:1], scalar2=rstd[:, j : j + 1],
+                    op0=ALU.subtract, op1=ALU.mult,
                 )
 
-        def transpose(g):
-            for h in range(HALVES):
-                transpose_half(g, h)
+        def transpose(j):
+            for half in range(HALVES):
+                y_t[(j, half)] = banks.tile([P, PACK, P], F32, tag="bank", name="y_t")
+                for t in range(PACK):
+                    nc.tensor.transpose(y_t[(j, half)][:, t, :], y[:, j, half, t, :], ident[:])
 
-        def gain_and_shift(g):
-            for kb in range(K_BLOCKS):
-                h, t = divmod(kb, PACK)
+        def gain_and_shift(j, half):
+            for t in range(PACK):
                 nc.scalar.activation(
-                    out=planes[:, g, h, t, :], in_=y_t[(g, h, t // BANK_BLOCKS)][:, t % BANK_BLOCKS, :],
-                    func=ACT.Identity, scale=gain[:, h, t : t + 1], bias=offset[:, h, t : t + 1],
+                    out=planes[:, j, t, P * half : P * (half + 1)], in_=y_t[(j, half)][:, t, :],
+                    func=ACT.Identity, scale=gain[:, half, t : t + 1], bias=offset[:, half, t : t + 1],
                 )
 
-        def regroup(g):
-            for h in range(HALVES):
-                nc.vector.tensor_copy(
-                    out=z_grouped[:, g, h].rearrange("p (c i) t -> p c t i", i=4),
-                    in_=planes[:, g, h].rearrange("p t (c i) -> p c t i", i=4),
-                )
+        def regroup(j):
+            nc.vector.tensor_copy(
+                out=z_grouped[:, j].rearrange("p (c i) t -> p c t i", i=4),
+                in_=planes[:, j].rearrange("p t (c i) -> p c t i", i=4),
+            )
 
-        def quantise(g):
-            for h in range(HALVES):
-                nc.vector.quantize_mx(
-                    out=z_codes[:, g, h, :].bitcast(FP8X4),
-                    scales=z_scales[:, g, h, :],
-                    in_=z_grouped[:, g, h].rearrange("p r t -> p (r t)"),
-                )
+        def quantise(j):
+            nc.vector.quantize_mx(
+                out=z_codes[:, j, :].bitcast(FP8X4),
+                scales=z_scales[:, j, :],
+                in_=z_grouped[:, j].rearrange("p r t -> p (r t)"),
+            )
 
-        def regroup_w(h):
+        def regroup_w(half):
             nc.gpsimd.tensor_scalar(
-                out=w_grouped[:, h].rearrange("p (c i) t -> p c t i", i=4),
-                in0=w_raw[:, PACK * h : PACK * (h + 1), :].rearrange("p t (c i) -> p c t i", i=4),
+                out=w_grouped[:, half].rearrange("p (c i) t -> p c t i", i=4),
+                in0=w_raw[:, PACK * half : PACK * (half + 1), :].rearrange("p t (c i) -> p c t i", i=4),
                 scalar1=1.0, scalar2=0.0, op0=ALU.mult, op1=ALU.add,
             )
 
@@ -192,64 +157,88 @@ def tile_textguidedcamfusion_pa_s_kernel(tc, pooled, proto, ln_g, ln_b, W, b, ou
                 in_=w_grouped[:].rearrange("p h d t -> p (h d t)"),
             )
 
-        def project(g):
-            acc[g] = products.tile([P, GROUP, D], F32, name="acc")
-            for e in range(GROUP):
-                rows = slice(P * e, P * (e + 1))
-                for h in range(HALVES):
-                    nc.tensor.matmul_mx(
-                        out=acc[g][:, e, :],
-                        lhsT=z_codes[:, g, h, rows].bitcast(FP8X4),
-                        lhsT_scale=z_scales[:, g, h, rows],
-                        rhs=w_codes[:, h, :].bitcast(FP8X4),
-                        rhs_scale=w_scales[:, h, :],
-                        start=(h == 0),
-                        stop=(h == HALVES - 1),
-                    )
+        def project(j):
+            acc[j] = products.tile([P, D], F32, name="acc")
+            for half in range(HALVES):
+                nc.tensor.matmul_mx(
+                    out=acc[j][:],
+                    lhsT=z_codes[:, j, P * half : P * (half + 1)].bitcast(FP8X4),
+                    lhsT_scale=z_scales[:, j, P * half : P * (half + 1)],
+                    rhs=w_codes[:, half, :].bitcast(FP8X4),
+                    rhs_scale=w_scales[:, half, :],
+                    start=(half == 0),
+                    stop=(half == HALVES - 1),
+                )
 
-        def add_bias(g):
-            nc.vector.tensor_tensor(
-                out=pre[:, cols_of(g), :], in0=acc[g][:],
-                in1=b_all[:].unsqueeze(1).to_broadcast([P, GROUP, D]), op=ALU.add,
-            )
+        def add_bias(j):
+            nc.vector.tensor_tensor(out=pre[:, j, :], in0=acc[j][:], in1=b_all[:], op=ALU.add)
 
-        def sum_squares(g):
-            for j in tiles_of(g):
-                squares = scratch.tile([P, D], F32)
+        def relu(j):
+            nc.scalar.activation(out=h[:, j, :], in_=pre[:, j, :], func=ACT.Relu)
+
+        def sum_squares(j):
+            if j < TILES - 1:
+                nc.scalar.activation(out=squares[:], in_=h[:, j, :], func=ACT.Square, accum_out=sumsq[:, j : j + 1])
+            else:
                 nc.vector.scalar_tensor_tensor(
-                    out=squares[:], in0=pre[:, j, :], scalar=0.0, in1=pre[:, j, :],
+                    out=result[:, j, :], in0=pre[:, j, :], scalar=0.0, in1=pre[:, j, :],
                     op0=ALU.max, op1=ALU.mult, accum_out=sumsq[:, j : j + 1],
                 )
 
-        def floor_sumsq(g):
-            nc.vector.tensor_scalar_max(out=norm[:, cols_of(g)], in0=sumsq[:, cols_of(g)], scalar1=1e-24)
+        def rnorm_of(j):
+            nc.scalar.activation(out=rnorm[:, j : j + 1], in_=sumsq[:, j : j + 1], func=ACT.Abs_reciprocal_sqrt)
 
-        def norm_of(g):
-            nc.scalar.sqrt(out=norm[:, cols_of(g)], in_=norm[:, cols_of(g)])
+        def scale_and_store(j):
+            engine = nc.gpsimd if j < TILES - 1 else nc.vector
+            engine.tensor_scalar(
+                out=rfloor[j][:], in0=rnorm[:, j : j + 1], scalar1=1e12, scalar2=0.0, op0=ALU.min, op1=ALU.add
+            )
+            engine.tensor_scalar(
+                out=result[:, j, :], in0=h[:, j, :], scalar1=rfloor[j][:], scalar2=0.0, op0=ALU.mult, op1=ALU.add
+            )
+            nc.sync.dma_start(out=out_rows[:, j, :], in_=result[:, j, :])
 
-        def rnorm_of(g):
-            nc.vector.reciprocal(out=rnorm[:, cols_of(g)], in_=norm[:, cols_of(g)])
+        c_bank = banks.tile([P, C], F32, tag="bank")
+        nc.tensor.matmul(out=c_bank[:], lhsT=mean_weights[:], rhs=proto_pad[:], start=True, stop=True)
+        row_stats(0)
+        nc.vector.bn_stats(out=stats[:, 0, PROTO, :], in_=c_bank[:])
+        join_stats(0)
+        rstd_of(0)
+        nc.scalar.copy(out=c_all[:], in_=c_bank[:].rearrange("p (q t) -> p t q", t=PACK))
+        row_stats(1)
+        nc.vector.tensor_copy(
+            out=stats[:, 1:TILES, PROTO, :], in_=stats[:, 0:1, PROTO, :].to_broadcast([P, TILES - 1, STATS])
+        )
+        join_stats(1)
+        rstd_of(1)
+        for half in range(HALVES):
+            regroup_w(half)
 
-        def scale_and_store(g):
-            for j in tiles_of(g):
-                nc.scalar.activation(out=result[:, j, :], in_=pre[:, j, :], func=ACT.Relu, scale=rnorm[:, j : j + 1])
-            nc.sync.dma_start(out=out_rows[:, cols_of(g), :], in_=result[:, cols_of(g), :])
+        def when(j, stage, *args):
+            if 0 <= j < TILES:
+                stage(j, *args)
 
-        nc.vector.bn_stats(out=c_stats[:], in_=c_bank[:])
-        nc.vector.tensor_copy(out=stats[:, :, PROTO, :], in_=c_stats[:].unsqueeze(1).to_broadcast([P, TILES, STATS]))
-        b_bank = banks.tile([P, D], F32, tag="bank")
-        nc.tensor.matmul(out=b_bank[:], lhsT=ones[:], rhs=bias_pad[:], start=True, stop=True)
-        nc.scalar.copy(out=b_all[:], in_=b_bank[:])
-        for h in range(HALVES):
-            regroup_w(h)
-        quantise_w()
-
-        stages = [
-            row_moments, join_moments, std_of, rstd_of, shift_of, normalise, transpose, gain_and_shift, regroup,
-            quantise, project, add_bias, sum_squares, floor_sumsq, norm_of, rnorm_of, scale_and_store,
-        ]
-        for wave in range(len(stages) + SKEW * (GROUPS - 1)):
-            for g in range(GROUPS):
-                s = wave - SKEW * g
-                if 0 <= s < len(stages):
-                    stages[s](g)
+        for n in range(-1, TILES + 4):
+            when(n - 4, rnorm_of)
+            when(n - 4, scale_and_store)
+            when(n + 1, normalise)
+            when(n + 1, transpose)
+            when(n, gain_and_shift, POOLED)
+            when(n + 3, row_stats)
+            when(n - 1, regroup)
+            when(n + 3, join_stats)
+            if n == 1:
+                b_bank = banks.tile([P, D], F32, tag="bank")
+                nc.tensor.matmul(out=b_bank[:], lhsT=ones[:], rhs=bias_pad[:], start=True, stop=True)
+                nc.scalar.copy(out=b_all[:], in_=b_bank[:])
+            if n == 2:
+                quantise_w()
+                project(0)
+            when(n - 2, add_bias)
+            when(n - 3, relu)
+            when(n, gain_and_shift, PROTO)
+            when(n + 3, rstd_of)
+            when(n - 3, sum_squares)
+            when(n - 1, quantise)
+            if n != 1:
+                when(n - 1, project)

@@ -20,8 +20,12 @@ POOLED, PROTO = 0, 1
 D = 256
 PROTOS = 64
 TILES = ROWS // P
+GROUPS = ((0,), (1, 2), (3, 4), (5, 6), (7,))
+LAST = len(GROUPS) - 1
+BANK = 512
 STATS = 6
 EPS = 1e-5
+W_PIECES = 4
 FLOPS = 2 * ROWS * HALVES * C * D
 
 
@@ -29,6 +33,7 @@ def tile_textguidedcamfusion_pa_s_kernel(tc, pooled, proto, ln_g, ln_b, W, b, ou
     nc = tc.nc
     with ExitStack() as ctx:
         keep = ctx.enter_context(tc.tile_pool(name="keep", bufs=1))
+        scratch = ctx.enter_context(tc.tile_pool(name="scratch", bufs=2))
         banks = ctx.enter_context(tc.psum_pool(name="banks", bufs=6))
         products = ctx.enter_context(tc.psum_pool(name="products", bufs=2))
         ctx.enter_context(tc.manual_schedule())
@@ -54,20 +59,20 @@ def tile_textguidedcamfusion_pa_s_kernel(tc, pooled, proto, ln_g, ln_b, W, b, ou
         g_raw = keep.tile([P, HALVES, PACK], BF16)
         s_raw = keep.tile([P, HALVES, PACK], BF16)
         bias_pad = keep.tile([P, D], BF16)
+        nc.scalar.dma_start(out=g_raw[:], in_=ln_g.rearrange("(h p t) -> p h t", p=P, t=PACK))
+        nc.scalar.dma_start(out=s_raw[:], in_=ln_b.rearrange("(h p t) -> p h t", p=P, t=PACK))
 
+        eps_col = keep.tile([P, 1], F32)
+        nc.vector.memset(eps_col[:], EPS)
         nc.vector.memset(proto_pad[PROTOS:P, :], 0.0)
         mean_weights = keep.tile([P, P], BF16)
         nc.vector.memset(mean_weights[:], 1.0 / PROTOS)
-        eps_col = keep.tile([P, 1], F32)
-        nc.vector.memset(eps_col[:], EPS)
         ones = keep.tile([P, P], BF16)
         nc.vector.memset(ones[:], 1.0)
         nc.vector.memset(bias_pad[:], 0.0)
-        nc.scalar.dma_start(out=g_raw[:], in_=ln_g.rearrange("(h p t) -> p h t", p=P, t=PACK))
-        nc.scalar.dma_start(out=s_raw[:], in_=ln_b.rearrange("(h p t) -> p h t", p=P, t=PACK))
-        nc.scalar.dma_start(out=bias_pad[0:1, :], in_=b.rearrange("(o d) -> o d", o=1))
         warm = keep.tile([P, 1], F32)
         nc.scalar.activation(out=warm[:], in_=eps_col[:], func=ACT.Abs_reciprocal_sqrt)
+        nc.scalar.dma_start(out=bias_pad[0:1, :], in_=b.rearrange("(o d) -> o d", o=1))
         ident = keep.tile([P, P], F32)
         make_identity(nc, ident[:])
         gain = keep.tile([P, HALVES, PACK], F32)
@@ -79,76 +84,104 @@ def tile_textguidedcamfusion_pa_s_kernel(tc, pooled, proto, ln_g, ln_b, W, b, ou
         stats = keep.tile([P, TILES, HALVES, STATS], F32)
         mean_var = keep.tile([P, TILES, 2], F32)
         rstd = keep.tile([P, TILES], F32)
+        shift = keep.tile([P, TILES], F32)
         y = keep.tile([P, TILES, HALVES, PACK, P], F32)
         y_t = {}
-        planes = keep.tile([P, TILES, PACK, HALVES * P], BF16)
-        z_grouped = keep.tile([P, TILES, HALVES * P, PACK], BF16, align_bytes=64)
-        z_codes = keep.tile([P, TILES, HALVES * P], U32, align_bytes=64)
-        z_scales = keep.tile([P, TILES, HALVES * P], U8, align_bytes=64)
+        planes, z_grouped, z_codes, z_scales, acc, sumsq, floored, rnorm = {}, {}, {}, {}, {}, {}, {}, {}
+        for g, tiles in enumerate(GROUPS):
+            rows = P * len(tiles)
+            planes[g] = keep.tile([P, HALVES, PACK, rows], BF16, name="planes_" + str(g))
+            z_grouped[g] = keep.tile([P, HALVES, rows, PACK], BF16, name="z_grouped_" + str(g), align_bytes=64)
+            z_codes[g] = keep.tile([P, HALVES, rows], U32, name="z_codes_" + str(g), align_bytes=64)
+            z_scales[g] = keep.tile([P, HALVES, rows], U8, name="z_scales_" + str(g), align_bytes=64)
+            sumsq[g] = keep.tile([P, len(tiles)], F32, name="sumsq_" + str(g))
+            floored[g] = keep.tile([P, len(tiles)], F32, name="floored_" + str(g))
+            rnorm[g] = keep.tile([P, len(tiles)], F32, name="rnorm_" + str(g))
         w_grouped = keep.tile([P, HALVES, D, PACK], BF16, align_bytes=64)
         w_codes = keep.tile([P, HALVES, D], U32, align_bytes=64)
         w_scales = keep.tile([P, HALVES, D], U8, align_bytes=64)
         b_all = keep.tile([P, D], F32)
-        acc = {}
         pre = keep.tile([P, TILES, D], F32)
-        h = keep.tile([P, TILES, D], F32)
-        squares = keep.tile([P, D], F32)
-        sumsq = keep.tile([P, TILES], F32)
-        rnorm = keep.tile([P, TILES], F32)
-        rfloor = {j: keep.tile([P, 1], F32, name="rfloor_" + str(j)) for j in range(TILES)}
         result = keep.tile([P, TILES, D], F32)
 
-        def row_stats(j):
-            nc.vector.bn_stats(out=stats[:, j, POOLED, :], in_=x[:, j, :])
+        def cols_of(g):
+            return slice(GROUPS[g][0], GROUPS[g][-1] + 1)
 
-        def join_stats(j):
-            nc.vector.bn_aggr(out=mean_var[:, j, :], in_=stats[:, j].rearrange("p h s -> p (h s)"))
+        def row_stats(g):
+            for j in GROUPS[g]:
+                nc.vector.bn_stats(out=stats[:, j, POOLED, :], in_=x[:, j, :])
 
-        def rstd_of(j):
+        def join_stats(g):
+            for j in GROUPS[g]:
+                nc.vector.bn_aggr(out=mean_var[:, j, :], in_=stats[:, j].rearrange("p h s -> p (h s)"))
+
+        def rstd_of(g):
             nc.scalar.activation(
-                out=rstd[:, j : j + 1], in_=mean_var[:, j, 1:2], func=ACT.Abs_reciprocal_sqrt, bias=eps_col[:]
+                out=rstd[:, cols_of(g)], in_=mean_var[:, cols_of(g), 1], func=ACT.Abs_reciprocal_sqrt, bias=eps_col[:]
             )
 
-        def normalise(j):
-            sources = (x[:, j, :].rearrange("p (q t) -> p t q", t=PACK), c_all[:])
-            for half in range(HALVES):
+        def shift_of(g):
+            nc.vector.scalar_tensor_tensor(
+                out=shift[:, cols_of(g)], in0=mean_var[:, cols_of(g), 0], scalar=-1.0, in1=rstd[:, cols_of(g)],
+                op0=ALU.mult, op1=ALU.mult,
+            )
+
+        def normalise_on_vector(g, half):
+            for j in GROUPS[g]:
+                source = c_all[:] if half == PROTO else x[:, j, :].rearrange("p (q t) -> p t q", t=PACK)
                 nc.vector.tensor_scalar(
-                    out=y[:, j, half], in0=sources[half], scalar1=mean_var[:, j, 0:1], scalar2=rstd[:, j : j + 1],
+                    out=y[:, j, half], in0=source, scalar1=mean_var[:, j, 0:1], scalar2=rstd[:, j : j + 1],
                     op0=ALU.subtract, op1=ALU.mult,
                 )
 
-        def transpose(j):
-            for half in range(HALVES):
-                y_t[(j, half)] = banks.tile([P, PACK, P], F32, tag="bank", name="y_t")
-                for t in range(PACK):
-                    nc.tensor.transpose(y_t[(j, half)][:, t, :], y[:, j, half, t, :], ident[:])
+        def normalise_on_scalar(g):
+            for j in GROUPS[g]:
+                nc.scalar.activation(
+                    out=y[:, j, POOLED], in_=x[:, j, :].rearrange("p (q t) -> p t q", t=PACK), func=ACT.Identity,
+                    scale=rstd[:, j : j + 1], bias=shift[:, j : j + 1],
+                )
 
-        def gain_and_shift(j, half):
+        def transpose(g, half):
+            rows = P * len(GROUPS[g])
+            blocks = BANK // rows
+            for t in range(PACK):
+                bank, slot = divmod(t, blocks)
+                if slot == 0:
+                    y_t[(g, half, bank)] = banks.tile([P, blocks, rows], F32, tag="bank", name="y_t")
+                for e, j in enumerate(GROUPS[g]):
+                    nc.tensor.transpose(
+                        y_t[(g, half, bank)][:, slot, P * e : P * (e + 1)], y[:, j, half, t, :], ident[:]
+                    )
+
+        def gain_and_shift(g, half):
+            blocks = BANK // (P * len(GROUPS[g]))
             for t in range(PACK):
                 nc.scalar.activation(
-                    out=planes[:, j, t, P * half : P * (half + 1)], in_=y_t[(j, half)][:, t, :],
+                    out=planes[g][:, half, t, :], in_=y_t[(g, half, t // blocks)][:, t % blocks, :],
                     func=ACT.Identity, scale=gain[:, half, t : t + 1], bias=offset[:, half, t : t + 1],
                 )
 
-        def regroup(j):
+        def regroup(g, half):
             nc.vector.tensor_copy(
-                out=z_grouped[:, j].rearrange("p (c i) t -> p c t i", i=4),
-                in_=planes[:, j].rearrange("p t (c i) -> p c t i", i=4),
+                out=z_grouped[g][:, half].rearrange("p (c i) t -> p c t i", i=4),
+                in_=planes[g][:, half].rearrange("p t (c i) -> p c t i", i=4),
             )
 
-        def quantise(j):
+        def quantise(g, half):
             nc.vector.quantize_mx(
-                out=z_codes[:, j, :].bitcast(FP8X4),
-                scales=z_scales[:, j, :],
-                in_=z_grouped[:, j].rearrange("p r t -> p (r t)"),
+                out=z_codes[g][:, half, :].bitcast(FP8X4),
+                scales=z_scales[g][:, half, :],
+                in_=z_grouped[g][:, half].rearrange("p r t -> p (r t)"),
             )
 
         def regroup_w(half):
-            nc.gpsimd.tensor_scalar(
-                out=w_grouped[:, half].rearrange("p (c i) t -> p c t i", i=4),
-                in0=w_raw[:, PACK * half : PACK * (half + 1), :].rearrange("p t (c i) -> p c t i", i=4),
-                scalar1=1.0, scalar2=0.0, op0=ALU.mult, op1=ALU.add,
-            )
+            width = HALVES * D // W_PIECES
+            for a in range(0, D, width):
+                nc.gpsimd.tensor_scalar(
+                    out=w_grouped[:, half, a : a + width].rearrange("p (c i) t -> p c t i", i=4),
+                    in0=w_raw[:, PACK * half : PACK * (half + 1), a : a + width].rearrange("p t (c i) -> p c t i", i=4),
+                    scalar1=1.0, scalar2=0.0, op0=ALU.mult, op1=ALU.add,
+                )
 
         def quantise_w():
             nc.vector.quantize_mx(
@@ -157,88 +190,99 @@ def tile_textguidedcamfusion_pa_s_kernel(tc, pooled, proto, ln_g, ln_b, W, b, ou
                 in_=w_grouped[:].rearrange("p h d t -> p (h d t)"),
             )
 
-        def project(j):
-            acc[j] = products.tile([P, D], F32, name="acc")
-            for half in range(HALVES):
-                nc.tensor.matmul_mx(
-                    out=acc[j][:],
-                    lhsT=z_codes[:, j, P * half : P * (half + 1)].bitcast(FP8X4),
-                    lhsT_scale=z_scales[:, j, P * half : P * (half + 1)],
-                    rhs=w_codes[:, half, :].bitcast(FP8X4),
-                    rhs_scale=w_scales[:, half, :],
-                    start=(half == 0),
-                    stop=(half == HALVES - 1),
-                )
+        def project(g):
+            acc[g] = products.tile([P, len(GROUPS[g]), D], F32, tag="product", name="acc")
+            for e in range(len(GROUPS[g])):
+                rows = slice(P * e, P * (e + 1))
+                for half in range(HALVES):
+                    nc.tensor.matmul_mx(
+                        out=acc[g][:, e, :],
+                        lhsT=z_codes[g][:, half, rows].bitcast(FP8X4),
+                        lhsT_scale=z_scales[g][:, half, rows],
+                        rhs=w_codes[:, half, :].bitcast(FP8X4),
+                        rhs_scale=w_scales[:, half, :],
+                        start=(half == 0),
+                        stop=(half == HALVES - 1),
+                    )
 
-        def add_bias(j):
-            nc.vector.tensor_tensor(out=pre[:, j, :], in0=acc[j][:], in1=b_all[:], op=ALU.add)
+        def add_bias(g):
+            nc.vector.tensor_tensor(
+                out=pre[:, cols_of(g), :], in0=acc[g][:],
+                in1=b_all[:].unsqueeze(1).to_broadcast([P, len(GROUPS[g]), D]), op=ALU.add,
+            )
 
-        def relu(j):
-            nc.scalar.activation(out=h[:, j, :], in_=pre[:, j, :], func=ACT.Relu)
-
-        def sum_squares(j):
-            if j < TILES - 1:
-                nc.scalar.activation(out=squares[:], in_=h[:, j, :], func=ACT.Square, accum_out=sumsq[:, j : j + 1])
-            else:
+        def sum_squares(g):
+            for e, j in enumerate(GROUPS[g]):
+                squares = scratch.tile([P, D], F32)
                 nc.vector.scalar_tensor_tensor(
-                    out=result[:, j, :], in0=pre[:, j, :], scalar=0.0, in1=pre[:, j, :],
-                    op0=ALU.max, op1=ALU.mult, accum_out=sumsq[:, j : j + 1],
+                    out=squares[:], in0=pre[:, j, :], scalar=0.0, in1=pre[:, j, :],
+                    op0=ALU.max, op1=ALU.mult, accum_out=sumsq[g][:, e : e + 1],
                 )
 
-        def rnorm_of(j):
-            nc.scalar.activation(out=rnorm[:, j : j + 1], in_=sumsq[:, j : j + 1], func=ACT.Abs_reciprocal_sqrt)
+        def floor_sumsq(g):
+            engine = nc.vector if g == LAST else nc.gpsimd
+            engine.tensor_scalar(
+                out=floored[g][:], in0=sumsq[g][:], scalar1=1e-24, scalar2=0.0, op0=ALU.max, op1=ALU.add
+            )
 
-        def scale_and_store(j):
-            engine = nc.gpsimd if j < TILES - 1 else nc.vector
-            engine.tensor_scalar(
-                out=rfloor[j][:], in0=rnorm[:, j : j + 1], scalar1=1e12, scalar2=0.0, op0=ALU.min, op1=ALU.add
-            )
-            engine.tensor_scalar(
-                out=result[:, j, :], in0=h[:, j, :], scalar1=rfloor[j][:], scalar2=0.0, op0=ALU.mult, op1=ALU.add
-            )
-            nc.sync.dma_start(out=out_rows[:, j, :], in_=result[:, j, :])
+        def rnorm_of(g):
+            nc.scalar.activation(out=rnorm[g][:], in_=floored[g][:], func=ACT.Abs_reciprocal_sqrt)
+
+        def scale_and_store(g):
+            for e, j in enumerate(GROUPS[g]):
+                nc.scalar.activation(out=result[:, j, :], in_=pre[:, j, :], func=ACT.Relu, scale=rnorm[g][:, e : e + 1])
+            nc.sync.dma_start(out=out_rows[:, cols_of(g), :], in_=result[:, cols_of(g), :])
 
         c_bank = banks.tile([P, C], F32, tag="bank")
         nc.tensor.matmul(out=c_bank[:], lhsT=mean_weights[:], rhs=proto_pad[:], start=True, stop=True)
         row_stats(0)
         nc.vector.bn_stats(out=stats[:, 0, PROTO, :], in_=c_bank[:])
-        join_stats(0)
-        rstd_of(0)
-        nc.scalar.copy(out=c_all[:], in_=c_bank[:].rearrange("p (q t) -> p t q", t=PACK))
-        row_stats(1)
         nc.vector.tensor_copy(
             out=stats[:, 1:TILES, PROTO, :], in_=stats[:, 0:1, PROTO, :].to_broadcast([P, TILES - 1, STATS])
         )
-        join_stats(1)
-        rstd_of(1)
+        join_stats(0)
+        rstd_of(0)
+        nc.scalar.copy(out=c_all[:], in_=c_bank[:].rearrange("p (q t) -> p t q", t=PACK))
         for half in range(HALVES):
             regroup_w(half)
 
-        def when(j, stage, *args):
-            if 0 <= j < TILES:
-                stage(j, *args)
+        def spread_bias():
+            b_bank = products.tile([P, D], F32, tag="product")
+            nc.tensor.matmul(out=b_bank[:], lhsT=ones[:], rhs=bias_pad[:], start=True, stop=True)
+            nc.scalar.copy(out=b_all[:], in_=b_bank[:])
 
-        for n in range(-1, TILES + 4):
-            when(n - 4, rnorm_of)
-            when(n - 4, scale_and_store)
-            when(n + 1, normalise)
-            when(n + 1, transpose)
-            when(n, gain_and_shift, POOLED)
-            when(n + 3, row_stats)
-            when(n - 1, regroup)
-            when(n + 3, join_stats)
-            if n == 1:
-                b_bank = banks.tile([P, D], F32, tag="bank")
-                nc.tensor.matmul(out=b_bank[:], lhsT=ones[:], rhs=bias_pad[:], start=True, stop=True)
-                nc.scalar.copy(out=b_all[:], in_=b_bank[:])
+        def when(g, stage, *args):
+            if 0 <= g <= LAST:
+                stage(g, *args)
+
+        for n in range(LAST + 6):
+            if n > 0:
+                when(n, row_stats)
+            when(n - 3, project)
+            when(n - 5, scale_and_store)
+            when(n - 1, transpose, PROTO)
+            when(n - 2, regroup, PROTO)
+            if n > 0:
+                when(n, join_stats)
+            when(n - 2, regroup, POOLED)
+            when(n - 3, add_bias)
+            when(n - 1, transpose, POOLED)
+            if n > 0:
+                when(n, rstd_of)
+            when(n - 4, floor_sumsq)
             if n == 2:
                 quantise_w()
-                project(0)
-            when(n - 2, add_bias)
-            when(n - 3, relu)
-            when(n, gain_and_shift, PROTO)
-            when(n + 3, rstd_of)
+            when(n - 2, quantise, POOLED)
+            when(n - 4, rnorm_of)
+            when(n - 1, gain_and_shift, PROTO)
+            if n == 1:
+                spread_bias()
+            when(n - 2, quantise, PROTO)
+            when(n - 1, gain_and_shift, POOLED)
+            if 0 < n < LAST:
+                shift_of(n)
+                normalise_on_scalar(n)
+            else:
+                when(n, normalise_on_vector, POOLED)
             when(n - 3, sum_squares)
-            when(n - 1, quantise)
-            if n != 1:
-                when(n - 1, project)
+            when(n, normalise_on_vector, PROTO)

@@ -48,14 +48,14 @@ def tile_textguidedcamfusion_pa_s_kernel(tc, pooled, proto, ln_g, ln_b, W, b, ou
             nc.sync.dma_start(out=x[:, a:z, :], in_=pooled_rows[:, a:z, :])
 
         load_x(0, 1)
-        load_x(1, 2)
+        load_x(1, 3)
         w_raw = keep.tile([P, HALVES * PACK, D], BF16)
         nc.sync.dma_start(
             out=w_raw[:].rearrange("p (h t) d -> p h (t d)", t=PACK),
             in_=W.rearrange("(h p t) d -> p h (t d)", p=P, t=PACK),
         )
-        load_x(2, 4)
-        load_x(4, TILES)
+        load_x(3, 5)
+        load_x(5, 8)
         g_raw = keep.tile([P, HALVES, PACK], BF16)
         s_raw = keep.tile([P, HALVES, PACK], BF16)
         bias_pad = keep.tile([P, D], BF16)
@@ -243,46 +243,43 @@ def tile_textguidedcamfusion_pa_s_kernel(tc, pooled, proto, ln_g, ln_b, W, b, ou
         join_stats(0)
         rstd_of(0)
         nc.scalar.copy(out=c_all[:], in_=c_bank[:].rearrange("p (q t) -> p t q", t=PACK))
+        row_stats(1)
         for half in range(HALVES):
             regroup_w(half)
 
-        def spread_bias():
-            b_bank = products.tile([P, D], F32, tag="product")
-            nc.tensor.matmul(out=b_bank[:], lhsT=ones[:], rhs=bias_pad[:], start=True, stop=True)
-            nc.scalar.copy(out=b_all[:], in_=b_bank[:])
+        b_bank = products.tile([P, D], F32, tag="product")
+        nc.tensor.matmul(out=b_bank[:], lhsT=ones[:], rhs=bias_pad[:], start=True, stop=True)
+        nc.scalar.copy(out=b_all[:], in_=b_bank[:])
 
         def when(g, stage, *args):
             if 0 <= g <= LAST:
                 stage(g, *args)
 
-        for n in range(LAST + 6):
-            if n > 0:
+        for n in range(1, LAST + 7):
+            when(n - 3, regroup, PROTO)
+            if n > 1:
                 when(n, row_stats)
-            when(n - 3, project)
-            when(n - 5, scale_and_store)
-            when(n - 1, transpose, PROTO)
-            when(n - 2, regroup, PROTO)
-            if n > 0:
-                when(n, join_stats)
-            when(n - 2, regroup, POOLED)
-            when(n - 3, add_bias)
-            when(n - 1, transpose, POOLED)
-            if n > 0:
-                when(n, rstd_of)
-            when(n - 4, floor_sumsq)
-            if n == 2:
+            when(n - 3, regroup, POOLED)
+            when(n, join_stats)
+            when(n - 4, add_bias)
+            if 0 < n - 1 < LAST:
+                shift_of(n - 1)
+            when(n - 2, gain_and_shift, PROTO)
+            when(n - 6, rnorm_of)
+            when(n - 3, quantise, POOLED)
+            when(n - 2, transpose, POOLED)
+            when(n - 3, quantise, PROTO)
+            if n == 3:
                 quantise_w()
-            when(n - 2, quantise, POOLED)
-            when(n - 4, rnorm_of)
-            when(n - 1, gain_and_shift, PROTO)
-            if n == 1:
-                spread_bias()
-            when(n - 2, quantise, PROTO)
-            when(n - 1, gain_and_shift, POOLED)
-            if 0 < n < LAST:
-                shift_of(n)
-                normalise_on_scalar(n)
+            when(n - 2, gain_and_shift, POOLED)
+            when(n - 1, normalise_on_vector, PROTO)
+            if 0 < n - 1 < LAST:
+                normalise_on_scalar(n - 1)
             else:
-                when(n, normalise_on_vector, POOLED)
-            when(n - 3, sum_squares)
-            when(n, normalise_on_vector, PROTO)
+                when(n - 1, normalise_on_vector, POOLED)
+            when(n, rstd_of)
+            when(n - 5, floor_sumsq)
+            when(n - 4, sum_squares)
+            when(n - 3, project)
+            when(n - 6, scale_and_store)
+            when(n - 1, transpose, PROTO)

@@ -22,6 +22,8 @@ PROTOS = 64
 TILES = ROWS // P
 GROUPS = ((0,), (1, 2), (3, 4), (5, 6), (7,))
 LAST = len(GROUPS) - 1
+SCALAR_SQUARES = (LAST - 2,)
+VECTOR_SCALES = (LAST - 1, LAST)
 BANK = 512
 STATS = 6
 EPS = 1e-5
@@ -58,7 +60,8 @@ def tile_textguidedcamfusion_pa_s_kernel(tc, pooled, proto, ln_g, ln_b, W, b, ou
         load_x(5, 8)
         g_raw = keep.tile([P, HALVES, PACK], BF16)
         s_raw = keep.tile([P, HALVES, PACK], BF16)
-        bias_pad = keep.tile([P, D], BF16)
+        b_all = keep.tile([P, D], BF16)
+        nc.sync.dma_start(out=b_all[:], in_=b.partition_broadcast(P))
         nc.scalar.dma_start(out=g_raw[:], in_=ln_g.rearrange("(h p t) -> p h t", p=P, t=PACK))
         nc.scalar.dma_start(out=s_raw[:], in_=ln_b.rearrange("(h p t) -> p h t", p=P, t=PACK))
 
@@ -67,12 +70,8 @@ def tile_textguidedcamfusion_pa_s_kernel(tc, pooled, proto, ln_g, ln_b, W, b, ou
         nc.vector.memset(proto_pad[PROTOS:P, :], 0.0)
         mean_weights = keep.tile([P, P], BF16)
         nc.vector.memset(mean_weights[:], 1.0 / PROTOS)
-        ones = keep.tile([P, P], BF16)
-        nc.vector.memset(ones[:], 1.0)
-        nc.vector.memset(bias_pad[:], 0.0)
         warm = keep.tile([P, 1], F32)
         nc.scalar.activation(out=warm[:], in_=eps_col[:], func=ACT.Abs_reciprocal_sqrt)
-        nc.scalar.dma_start(out=bias_pad[0:1, :], in_=b.rearrange("(o d) -> o d", o=1))
         ident = keep.tile([P, P], F32)
         make_identity(nc, ident[:])
         gain = keep.tile([P, HALVES, PACK], F32)
@@ -100,8 +99,8 @@ def tile_textguidedcamfusion_pa_s_kernel(tc, pooled, proto, ln_g, ln_b, W, b, ou
         w_grouped = keep.tile([P, HALVES, D, PACK], BF16, align_bytes=64)
         w_codes = keep.tile([P, HALVES, D], U32, align_bytes=64)
         w_scales = keep.tile([P, HALVES, D], U8, align_bytes=64)
-        b_all = keep.tile([P, D], F32)
         pre = keep.tile([P, TILES, D], F32)
+        h = keep.tile([P, TILES, D], F32)
         result = keep.tile([P, TILES, D], F32)
 
         def cols_of(g):
@@ -212,6 +211,14 @@ def tile_textguidedcamfusion_pa_s_kernel(tc, pooled, proto, ln_g, ln_b, W, b, ou
             )
 
         def sum_squares(g):
+            if g in SCALAR_SQUARES:
+                nc.scalar.activation(out=h[:, cols_of(g), :], in_=pre[:, cols_of(g), :], func=ACT.Relu)
+                for e, j in enumerate(GROUPS[g]):
+                    squares = scratch.tile([P, D], F32)
+                    nc.scalar.activation(
+                        out=squares[:], in_=h[:, j, :], func=ACT.Square, accum_out=sumsq[g][:, e : e + 1]
+                    )
+                return
             for e, j in enumerate(GROUPS[g]):
                 squares = scratch.tile([P, D], F32)
                 nc.vector.scalar_tensor_tensor(
@@ -230,7 +237,15 @@ def tile_textguidedcamfusion_pa_s_kernel(tc, pooled, proto, ln_g, ln_b, W, b, ou
 
         def scale_and_store(g):
             for e, j in enumerate(GROUPS[g]):
-                nc.scalar.activation(out=result[:, j, :], in_=pre[:, j, :], func=ACT.Relu, scale=rnorm[g][:, e : e + 1])
+                if g in VECTOR_SCALES:
+                    nc.vector.tensor_scalar(
+                        out=result[:, j, :], in0=pre[:, j, :], scalar1=rnorm[g][:, e : e + 1], scalar2=0.0,
+                        op0=ALU.mult, op1=ALU.max,
+                    )
+                else:
+                    nc.scalar.activation(
+                        out=result[:, j, :], in_=pre[:, j, :], func=ACT.Relu, scale=rnorm[g][:, e : e + 1]
+                    )
             nc.sync.dma_start(out=out_rows[:, cols_of(g), :], in_=result[:, cols_of(g), :])
 
         c_bank = banks.tile([P, C], F32, tag="bank")
@@ -247,9 +262,6 @@ def tile_textguidedcamfusion_pa_s_kernel(tc, pooled, proto, ln_g, ln_b, W, b, ou
         for half in range(HALVES):
             regroup_w(half)
 
-        b_bank = products.tile([P, D], F32, tag="product")
-        nc.tensor.matmul(out=b_bank[:], lhsT=ones[:], rhs=bias_pad[:], start=True, stop=True)
-        nc.scalar.copy(out=b_all[:], in_=b_bank[:])
 
         def when(g, stage, *args):
             if 0 <= g <= LAST:
@@ -261,7 +273,8 @@ def tile_textguidedcamfusion_pa_s_kernel(tc, pooled, proto, ln_g, ln_b, W, b, ou
                 when(n, row_stats)
             when(n - 3, regroup, POOLED)
             when(n, join_stats)
-            when(n - 4, add_bias)
+            if n - 3 < LAST:
+                when(n - 4, add_bias)
             if 0 < n - 1 < LAST:
                 shift_of(n - 1)
             when(n - 2, gain_and_shift, PROTO)
@@ -269,6 +282,9 @@ def tile_textguidedcamfusion_pa_s_kernel(tc, pooled, proto, ln_g, ln_b, W, b, ou
             when(n - 3, quantise, POOLED)
             when(n - 2, transpose, POOLED)
             when(n - 3, quantise, PROTO)
+            if n - 3 >= LAST:
+                when(n - 3, project)
+                when(n - 4, add_bias)
             if n == 3:
                 quantise_w()
             when(n - 2, gain_and_shift, POOLED)
@@ -280,6 +296,7 @@ def tile_textguidedcamfusion_pa_s_kernel(tc, pooled, proto, ln_g, ln_b, W, b, ou
             when(n, rstd_of)
             when(n - 5, floor_sumsq)
             when(n - 4, sum_squares)
-            when(n - 3, project)
+            if n - 3 < LAST:
+                when(n - 3, project)
             when(n - 6, scale_and_store)
             when(n - 1, transpose, PROTO)

@@ -175,6 +175,12 @@ def tile_textguidedcamfusion_pa_s_kernel(tc, pooled, proto, ln_g, ln_b, W, b, ou
 
         def regroup_w(half):
             width = HALVES * D // W_PIECES
+            if half == 0:
+                nc.scalar.copy(
+                    out=w_grouped[:, half].rearrange("p (c i) t -> p c t i", i=4),
+                    in_=w_raw[:, PACK * half : PACK * (half + 1), :].rearrange("p t (c i) -> p c t i", i=4),
+                )
+                return
             for a in range(0, D, width):
                 nc.gpsimd.tensor_scalar(
                     out=w_grouped[:, half, a : a + width].rearrange("p (c i) t -> p c t i", i=4),

@@ -120,10 +120,11 @@ def tile_textguidedcamfusion_pa_s_kernel(tc, pooled, proto, ln_g, ln_b, W, b, ou
             )
 
         def shift_of(g):
-            nc.vector.scalar_tensor_tensor(
-                out=shift[:, cols_of(g)], in0=mean_var[:, cols_of(g), 0], scalar=-1.0, in1=rstd[:, cols_of(g)],
-                op0=ALU.mult, op1=ALU.mult,
-            )
+            for j in GROUPS[g]:
+                nc.gpsimd.tensor_scalar(
+                    out=shift[:, j : j + 1], in0=mean_var[:, j, 0:1], scalar1=rstd[:, j : j + 1], scalar2=-1.0,
+                    op0=ALU.mult, op1=ALU.mult,
+                )
 
         def normalise_on_vector(g, half):
             for j in GROUPS[g]:
@@ -258,7 +259,7 @@ def tile_textguidedcamfusion_pa_s_kernel(tc, pooled, proto, ln_g, ln_b, W, b, ou
         nc.tensor.matmul(out=c_bank[:], lhsT=mean_weights[:], rhs=proto_pad[:], start=True, stop=True)
         row_stats(0)
         nc.vector.bn_stats(out=stats[:, 0, PROTO, :], in_=c_bank[:])
-        nc.vector.tensor_copy(
+        nc.scalar.copy(
             out=stats[:, 1:TILES, PROTO, :], in_=stats[:, 0:1, PROTO, :].to_broadcast([P, TILES - 1, STATS])
         )
         join_stats(0)
@@ -281,7 +282,7 @@ def tile_textguidedcamfusion_pa_s_kernel(tc, pooled, proto, ln_g, ln_b, W, b, ou
             when(n, join_stats)
             if n - 3 < LAST:
                 when(n - 4, add_bias)
-            if 0 < n - 1 < LAST:
+            if 0 < n - 1 <= LAST:
                 shift_of(n - 1)
             when(n - 2, gain_and_shift, PROTO)
             when(n - 6, rnorm_of)
@@ -295,7 +296,7 @@ def tile_textguidedcamfusion_pa_s_kernel(tc, pooled, proto, ln_g, ln_b, W, b, ou
                 quantise_w()
             when(n - 2, gain_and_shift, POOLED)
             when(n - 1, normalise_on_vector, PROTO)
-            if 0 < n - 1 < LAST:
+            if 0 < n - 1 <= LAST:
                 normalise_on_scalar(n - 1)
             else:
                 when(n - 1, normalise_on_vector, POOLED)

@@ -234,7 +234,7 @@ def tile_textguidedcamfusion_pa_s_kernel(tc, pooled, proto, ln_g, ln_b, W, b, ou
                 )
 
         def floor_sumsq(g):
-            engine = nc.vector if g == LAST else nc.gpsimd
+            engine = nc.vector if g >= LAST - 1 else nc.gpsimd
             engine.tensor_scalar(
                 out=floored[g][:], in0=sumsq[g][:], scalar1=1e-24, scalar2=0.0, op0=ALU.max, op1=ALU.add
             )
@@ -249,11 +249,13 @@ def tile_textguidedcamfusion_pa_s_kernel(tc, pooled, proto, ln_g, ln_b, W, b, ou
                         out=result[:, j, :], in0=pre[:, j, :], scalar1=rnorm[g][:, e : e + 1], scalar2=0.0,
                         op0=ALU.mult, op1=ALU.max,
                     )
+                    nc.sync.dma_start(out=out_rows[:, j : j + 1, :], in_=result[:, j : j + 1, :])
                 else:
                     nc.scalar.activation(
                         out=result[:, j, :], in_=pre[:, j, :], func=ACT.Relu, scale=rnorm[g][:, e : e + 1]
                     )
-            nc.sync.dma_start(out=out_rows[:, cols_of(g), :], in_=result[:, cols_of(g), :])
+            if g not in VECTOR_SCALES:
+                nc.sync.dma_start(out=out_rows[:, cols_of(g), :], in_=result[:, cols_of(g), :])
 
         c_bank = banks.tile([P, C], F32, tag="bank")
         nc.tensor.matmul(out=c_bank[:], lhsT=mean_weights[:], rhs=proto_pad[:], start=True, stop=True)
@@ -286,9 +288,12 @@ def tile_textguidedcamfusion_pa_s_kernel(tc, pooled, proto, ln_g, ln_b, W, b, ou
                 shift_of(n - 1)
             when(n - 2, gain_and_shift, PROTO)
             when(n - 6, rnorm_of)
+            if n - 3 == LAST:
+                quantise(LAST, PROTO)
             when(n - 3, quantise, POOLED)
             when(n - 2, transpose, POOLED)
-            when(n - 3, quantise, PROTO)
+            if n - 3 < LAST:
+                when(n - 3, quantise, PROTO)
             if n - 3 >= LAST:
                 when(n - 3, project)
                 when(n - 4, add_bias)

@@ -19,6 +19,7 @@ HALVES = 2
 POOLED, PROTO = 0, 1
 D = 256
 PROTOS = 64
+SIDES = P // PROTOS
 TILES = ROWS // P
 GROUPS = ((0,), (1, 2), (3, 4), (5, 6), (7,))
 LAST = len(GROUPS) - 1
@@ -40,8 +41,12 @@ def tile_textguidedcamfusion_pa_s_kernel(tc, pooled, proto, ln_g, ln_b, W, b, ou
         products = ctx.enter_context(tc.psum_pool(name="products", bufs=2))
         ctx.enter_context(tc.manual_schedule())
 
-        proto_pad = keep.tile([P, C], BF16)
-        nc.sync.dma_start(out=proto_pad[0:PROTOS, :], in_=proto)
+        proto_wide = keep.tile([P, C // SIDES], BF16)
+        for side in range(SIDES):
+            nc.sync.dma_start(
+                out=proto_wide[PROTOS * side : PROTOS * (side + 1), :],
+                in_=proto[:, C // SIDES * side : C // SIDES * (side + 1)],
+            )
         x = keep.tile([P, TILES, C], BF16)
         pooled_rows = pooled.rearrange("(p j) c -> p j c", j=TILES)
         out_rows = out.rearrange("(p j) d -> p j d", j=TILES)
@@ -51,6 +56,10 @@ def tile_textguidedcamfusion_pa_s_kernel(tc, pooled, proto, ln_g, ln_b, W, b, ou
 
         load_x(0, 1)
         load_x(1, 3)
+        g_raw = keep.tile([P, HALVES, PACK], BF16)
+        s_raw = keep.tile([P, HALVES, PACK], BF16)
+        nc.sync.dma_start(out=g_raw[:], in_=ln_g.rearrange("(h p t) -> p h t", p=P, t=PACK))
+        nc.sync.dma_start(out=s_raw[:], in_=ln_b.rearrange("(h p t) -> p h t", p=P, t=PACK))
         w_raw = keep.tile([P, HALVES * PACK, D], BF16)
         nc.sync.dma_start(
             out=w_raw[:].rearrange("p (h t) d -> p h (t d)", t=PACK),
@@ -58,18 +67,17 @@ def tile_textguidedcamfusion_pa_s_kernel(tc, pooled, proto, ln_g, ln_b, W, b, ou
         )
         load_x(3, 5)
         load_x(5, 8)
-        g_raw = keep.tile([P, HALVES, PACK], BF16)
-        s_raw = keep.tile([P, HALVES, PACK], BF16)
         b_all = keep.tile([P, D], BF16)
         nc.sync.dma_start(out=b_all[:], in_=b.partition_broadcast(P))
-        nc.scalar.dma_start(out=g_raw[:], in_=ln_g.rearrange("(h p t) -> p h t", p=P, t=PACK))
-        nc.scalar.dma_start(out=s_raw[:], in_=ln_b.rearrange("(h p t) -> p h t", p=P, t=PACK))
 
         eps_col = keep.tile([P, 1], F32)
         nc.vector.memset(eps_col[:], EPS)
-        nc.vector.memset(proto_pad[PROTOS:P, :], 0.0)
-        mean_weights = keep.tile([P, P], BF16)
-        nc.vector.memset(mean_weights[:], 1.0 / PROTOS)
+        mean_weights = keep.tile([P, SIDES, P], BF16)
+        for side in range(SIDES):
+            for rows in range(SIDES):
+                nc.vector.memset(
+                    mean_weights[PROTOS * rows : PROTOS * (rows + 1), side, :], 1.0 / PROTOS if rows == side else 0.0
+                )
         warm = keep.tile([P, 1], F32)
         nc.scalar.activation(out=warm[:], in_=eps_col[:], func=ACT.Abs_reciprocal_sqrt)
         ident = keep.tile([P, P], F32)
@@ -258,7 +266,11 @@ def tile_textguidedcamfusion_pa_s_kernel(tc, pooled, proto, ln_g, ln_b, W, b, ou
                 nc.sync.dma_start(out=out_rows[:, cols_of(g), :], in_=result[:, cols_of(g), :])
 
         c_bank = banks.tile([P, C], F32, tag="bank")
-        nc.tensor.matmul(out=c_bank[:], lhsT=mean_weights[:], rhs=proto_pad[:], start=True, stop=True)
+        for side in range(SIDES):
+            nc.tensor.matmul(
+                out=c_bank[:, C // SIDES * side : C // SIDES * (side + 1)], lhsT=mean_weights[:, side, :],
+                rhs=proto_wide[:], start=True, stop=True,
+            )
         row_stats(0)
         nc.vector.bn_stats(out=stats[:, 0, PROTO, :], in_=c_bank[:])
         nc.scalar.copy(

from contextlib import ExitStack

import concourse.mybir as mybir
from concourse.masks import make_identity

F32 = mybir.dt.float32
BF16 = mybir.dt.bfloat16
U32 = mybir.dt.uint32
U8 = mybir.dt.uint8
FP8X4 = mybir.dt.float8_e4m3fn_x4
ALU = mybir.AluOpType
ACT = mybir.ActivationFunctionType

P = 128
PACK = 4
ROWS = 1024
C = 512
HALVES = 2
POOLED, PROTO = 0, 1
D = 256
PROTOS = 64
SIDES = P // PROTOS
TILES = ROWS // P
GROUPS = ((0,), (1, 2), (3, 4), (5, 6), (7,))
LAST = len(GROUPS) - 1
SCALAR_SQUARES = (LAST - 2,)
VECTOR_SCALES = (LAST - 1, LAST)
BANK = 512
STATS = 6
EPS = 1e-5
W_PIECES = 4
FLOPS = 2 * ROWS * HALVES * C * D


def tile_textguidedcamfusion_pa_s_kernel(tc, pooled, proto, ln_g, ln_b, W, b, out):
    nc = tc.nc
    with ExitStack() as ctx:
        keep = ctx.enter_context(tc.tile_pool(name="keep", bufs=1))
        scratch = ctx.enter_context(tc.tile_pool(name="scratch", bufs=2))
        banks = ctx.enter_context(tc.psum_pool(name="banks", bufs=6))
        products = ctx.enter_context(tc.psum_pool(name="products", bufs=2))
        ctx.enter_context(tc.manual_schedule())

        proto_wide = keep.tile([P, C // SIDES], BF16)
        for side in range(SIDES):
            nc.sync.dma_start(
                out=proto_wide[PROTOS * side : PROTOS * (side + 1), :],
                in_=proto[:, C // SIDES * side : C // SIDES * (side + 1)],
            )
        x = keep.tile([P, TILES, C], BF16)
        pooled_rows = pooled.rearrange("(p j) c -> p j c", j=TILES)
        out_rows = out.rearrange("(p j) d -> p j d", j=TILES)

        def load_x(a, z):
            nc.sync.dma_start(out=x[:, a:z, :], in_=pooled_rows[:, a:z, :])

        load_x(0, 1)
        load_x(1, 3)
        g_raw = keep.tile([P, HALVES, PACK], BF16)
        s_raw = keep.tile([P, HALVES, PACK], BF16)
        nc.sync.dma_start(out=g_raw[:], in_=ln_g.rearrange("(h p t) -> p h t", p=P, t=PACK))
        nc.sync.dma_start(out=s_raw[:], in_=ln_b.rearrange("(h p t) -> p h t", p=P, t=PACK))
        w_raw = keep.tile([P, HALVES * PACK, D], BF16)
        nc.sync.dma_start(
            out=w_raw[:].rearrange("p (h t) d -> p h (t d)", t=PACK),
            in_=W.rearrange("(h p t) d -> p h (t d)", p=P, t=PACK),
        )
        load_x(3, 5)
        load_x(5, 8)
        b_all = keep.tile([P, D], BF16)
        nc.sync.dma_start(out=b_all[:], in_=b.partition_broadcast(P))

        eps_col = keep.tile([P, 1], F32)
        nc.vector.memset(eps_col[:], EPS)
        mean_weights = keep.tile([P, SIDES, P], BF16)
        for side in range(SIDES):
            for rows in range(SIDES):
                nc.vector.memset(
                    mean_weights[PROTOS * rows : PROTOS * (rows + 1), side, :], 1.0 / PROTOS if rows == side else 0.0
                )
        warm = keep.tile([P, 1], F32)
        nc.scalar.activation(out=warm[:], in_=eps_col[:], func=ACT.Abs_reciprocal_sqrt)
        ident = keep.tile([P, P], F32)
        make_identity(nc, ident[:])
        gain = keep.tile([P, HALVES, PACK], F32)
        offset = keep.tile([P, HALVES, PACK], F32)
        nc.gpsimd.tensor_copy(out=gain[:], in_=g_raw[:])
        nc.gpsimd.tensor_copy(out=offset[:], in_=s_raw[:])

        c_all = keep.tile([P, PACK, P], F32)
        stats = keep.tile([P, TILES, HALVES, STATS], F32)
        mean_var = keep.tile([P, TILES, 2], F32)
        rstd = keep.tile([P, TILES], F32)
        shift = keep.tile([P, TILES], F32)
        y = keep.tile([P, TILES, HALVES, PACK, P], F32)
        y_t = {}
        planes, z_grouped, z_codes, z_scales, acc, sumsq, floored, rnorm = {}, {}, {}, {}, {}, {}, {}, {}
        for g, tiles in enumerate(GROUPS):
            rows = P * len(tiles)
            planes[g] = keep.tile([P, HALVES, PACK, rows], BF16, name="planes_" + str(g))
            z_grouped[g] = keep.tile([P, HALVES, rows, PACK], BF16, name="z_grouped_" + str(g), align_bytes=64)
            z_codes[g] = keep.tile([P, HALVES, rows], U32, name="z_codes_" + str(g), align_bytes=64)
            z_scales[g] = keep.tile([P, HALVES, rows], U8, name="z_scales_" + str(g), align_bytes=64)
            sumsq[g] = keep.tile([P, len(tiles)], F32, name="sumsq_" + str(g))
            floored[g] = keep.tile([P, len(tiles)], F32, name="floored_" + str(g))
            rnorm[g] = keep.tile([P, len(tiles)], F32, name="rnorm_" + str(g))
        w_grouped = keep.tile([P, HALVES, D, PACK], BF16, align_bytes=64)
        w_codes = keep.tile([P, HALVES, D], U32, align_bytes=64)
        w_scales = keep.tile([P, HALVES, D], U8, align_bytes=64)
        pre = keep.tile([P, TILES, D], F32)
        h = keep.tile([P, TILES, D], F32)
        result = keep.tile([P, TILES, D], F32)

        def cols_of(g):
            return slice(GROUPS[g][0], GROUPS[g][-1] + 1)

        def row_stats(g):
            for j in GROUPS[g]:
                nc.vector.bn_stats(out=stats[:, j, POOLED, :], in_=x[:, j, :])

        def join_stats(g):
            for j in GROUPS[g]:
                nc.vector.bn_aggr(out=mean_var[:, j, :], in_=stats[:, j].rearrange("p h s -> p (h s)"))

        def rstd_of(g):
            nc.scalar.activation(
                out=rstd[:, cols_of(g)], in_=mean_var[:, cols_of(g), 1], func=ACT.Abs_reciprocal_sqrt, bias=eps_col[:]
            )

        def shift_of(g):
            for j in GROUPS[g]:
                nc.gpsimd.tensor_scalar(
                    out=shift[:, j : j + 1], in0=mean_var[:, j, 0:1], scalar1=rstd[:, j : j + 1], scalar2=-1.0,
                    op0=ALU.mult, op1=ALU.mult,
                )

        def normalise_on_vector(g, half):
            for j in GROUPS[g]:
                source = c_all[:] if half == PROTO else x[:, j, :].rearrange("p (q t) -> p t q", t=PACK)
                nc.vector.tensor_scalar(
                    out=y[:, j, half], in0=source, scalar1=mean_var[:, j, 0:1], scalar2=rstd[:, j : j + 1],
                    op0=ALU.subtract, op1=ALU.mult,
                )

        def normalise_on_scalar(g):
            for j in GROUPS[g]:
                nc.scalar.activation(
                    out=y[:, j, POOLED], in_=x[:, j, :].rearrange("p (q t) -> p t q", t=PACK), func=ACT.Identity,
                    scale=rstd[:, j : j + 1], bias=shift[:, j : j + 1],
                )

        def transpose(g, half):
            rows = P * len(GROUPS[g])
            blocks = BANK // rows
            for t in range(PACK):
                bank, slot = divmod(t, blocks)
                if slot == 0:
                    y_t[(g, half, bank)] = banks.tile([P, blocks, rows], F32, tag="bank", name="y_t")
                for e, j in enumerate(GROUPS[g]):
                    nc.tensor.transpose(
                        y_t[(g, half, bank)][:, slot, P * e : P * (e + 1)], y[:, j, half, t, :], ident[:]
                    )

        def gain_and_shift(g, half):
            blocks = BANK // (P * len(GROUPS[g]))
            for t in range(PACK):
                nc.scalar.activation(
                    out=planes[g][:, half, t, :], in_=y_t[(g, half, t // blocks)][:, t % blocks, :],
                    func=ACT.Identity, scale=gain[:, half, t : t + 1], bias=offset[:, half, t : t + 1],
                )

        def regroup(g, half):
            nc.vector.tensor_copy(
                out=z_grouped[g][:, half].rearrange("p (c i) t -> p c t i", i=4),
                in_=planes[g][:, half].rearrange("p t (c i) -> p c t i", i=4),
            )

        def quantise(g, half):
            nc.vector.quantize_mx(
                out=z_codes[g][:, half, :].bitcast(FP8X4),
                scales=z_scales[g][:, half, :],
                in_=z_grouped[g][:, half].rearrange("p r t -> p (r t)"),
            )

        def regroup_w(half):
            width = HALVES * D // W_PIECES
            if half == 0:
                nc.scalar.copy(
                    out=w_grouped[:, half].rearrange("p (c i) t -> p c t i", i=4),
                    in_=w_raw[:, PACK * half : PACK * (half + 1), :].rearrange("p t (c i) -> p c t i", i=4),
                )
                return
            for a in range(0, D, width):
                nc.gpsimd.tensor_scalar(
                    out=w_grouped[:, half, a : a + width].rearrange("p (c i) t -> p c t i", i=4),
                    in0=w_raw[:, PACK * half : PACK * (half + 1), a : a + width].rearrange("p t (c i) -> p c t i", i=4),
                    scalar1=1.0, scalar2=0.0, op0=ALU.mult, op1=ALU.add,
                )

        def quantise_w():
            nc.vector.quantize_mx(
                out=w_codes[:].rearrange("p h d -> p (h d)").bitcast(FP8X4),
                scales=w_scales[:].rearrange("p h d -> p (h d)"),
                in_=w_grouped[:].rearrange("p h d t -> p (h d t)"),
            )

        def project(g):
            acc[g] = products.tile([P, len(GROUPS[g]), D], F32, tag="product", name="acc")
            for e in range(len(GROUPS[g])):
                rows = slice(P * e, P * (e + 1))
                for half in range(HALVES):
                    nc.tensor.matmul_mx(
                        out=acc[g][:, e, :],
                        lhsT=z_codes[g][:, half, rows].bitcast(FP8X4),
                        lhsT_scale=z_scales[g][:, half, rows],
                        rhs=w_codes[:, half, :].bitcast(FP8X4),
                        rhs_scale=w_scales[:, half, :],
                        start=(half == 0),
                        stop=(half == HALVES - 1),
                    )

        def add_bias(g):
            nc.vector.tensor_tensor(
                out=pre[:, cols_of(g), :], in0=acc[g][:],
                in1=b_all[:].unsqueeze(1).to_broadcast([P, len(GROUPS[g]), D]), op=ALU.add,
            )

        def sum_squares(g):
            if g in SCALAR_SQUARES:
                nc.scalar.activation(out=h[:, cols_of(g), :], in_=pre[:, cols_of(g), :], func=ACT.Relu)
                for e, j in enumerate(GROUPS[g]):
                    squares = scratch.tile([P, D], F32)
                    nc.scalar.activation(
                        out=squares[:], in_=h[:, j, :], func=ACT.Square, accum_out=sumsq[g][:, e : e + 1]
                    )
                return
            for e, j in enumerate(GROUPS[g]):
                squares = scratch.tile([P, D], F32)
                nc.vector.scalar_tensor_tensor(
                    out=squares[:], in0=pre[:, j, :], scalar=0.0, in1=pre[:, j, :],
                    op0=ALU.max, op1=ALU.mult, accum_out=sumsq[g][:, e : e + 1],
                )

        def floor_sumsq(g):
            engine = nc.vector if g >= LAST - 1 else nc.gpsimd
            engine.tensor_scalar(
                out=floored[g][:], in0=sumsq[g][:], scalar1=1e-24, scalar2=0.0, op0=ALU.max, op1=ALU.add
            )

        def rnorm_of(g):
            nc.scalar.activation(out=rnorm[g][:], in_=floored[g][:], func=ACT.Abs_reciprocal_sqrt)

        def scale_and_store(g):
            for e, j in enumerate(GROUPS[g]):
                if g in VECTOR_SCALES:
                    nc.vector.tensor_scalar(
                        out=result[:, j, :], in0=pre[:, j, :], scalar1=rnorm[g][:, e : e + 1], scalar2=0.0,
                        op0=ALU.mult, op1=ALU.max,
                    )
                    nc.sync.dma_start(out=out_rows[:, j : j + 1, :], in_=result[:, j : j + 1, :])
                else:
                    nc.scalar.activation(
                        out=result[:, j, :], in_=pre[:, j, :], func=ACT.Relu, scale=rnorm[g][:, e : e + 1]
                    )
            if g not in VECTOR_SCALES:
                nc.sync.dma_start(out=out_rows[:, cols_of(g), :], in_=result[:, cols_of(g), :])

        c_bank = banks.tile([P, C], F32, tag="bank")
        for side in range(SIDES):
            nc.tensor.matmul(
                out=c_bank[:, C // SIDES * side : C // SIDES * (side + 1)], lhsT=mean_weights[:, side, :],
                rhs=proto_wide[:], start=True, stop=True,
            )
        row_stats(0)
        nc.vector.bn_stats(out=stats[:, 0, PROTO, :], in_=c_bank[:])
        nc.scalar.copy(
            out=stats[:, 1:TILES, PROTO, :], in_=stats[:, 0:1, PROTO, :].to_broadcast([P, TILES - 1, STATS])
        )
        join_stats(0)
        rstd_of(0)
        nc.scalar.copy(out=c_all[:], in_=c_bank[:].rearrange("p (q t) -> p t q", t=PACK))
        row_stats(1)
        for half in range(HALVES):
            regroup_w(half)


        def when(g, stage, *args):
            if 0 <= g <= LAST:
                stage(g, *args)

        for n in range(1, LAST + 7):
            when(n - 3, regroup, PROTO)
            if n > 1:
                when(n, row_stats)
            when(n - 3, regroup, POOLED)
            when(n, join_stats)
            if n - 3 < LAST:
                when(n - 4, add_bias)
            if 0 < n - 1 <= LAST:
                shift_of(n - 1)
            when(n - 2, gain_and_shift, PROTO)
            when(n - 6, rnorm_of)
            if n - 3 == LAST:
                quantise(LAST, PROTO)
            when(n - 3, quantise, POOLED)
            when(n - 2, transpose, POOLED)
            if n - 3 < LAST:
                when(n - 3, quantise, PROTO)
            if n - 3 >= LAST:
                when(n - 3, project)
                when(n - 4, add_bias)
            if n == 3:
                quantise_w()
            when(n - 2, gain_and_shift, POOLED)
            when(n - 1, normalise_on_vector, PROTO)
            if 0 < n - 1 <= LAST:
                normalise_on_scalar(n - 1)
            else:
                when(n - 1, normalise_on_vector, POOLED)
            when(n, rstd_of)
            when(n - 5, floor_sumsq)
            when(n - 4, sum_squares)
            if n - 3 < LAST:
                when(n - 3, project)
            when(n - 6, scale_and_store)
            when(n - 1, transpose, PROTO)
